import numpy as np
import ml_dtypes


def mxq(x, axis, fmt="e4m3"):
    dtype, down = {"e4m3": (ml_dtypes.float8_e4m3fn, 7), "e5m2": (ml_dtypes.float8_e5m2, 14)}[fmt]
    v = np.moveaxis(np.asarray(x, np.float32).astype(ml_dtypes.bfloat16).astype(np.float64), axis, -1)
    blocks = v.reshape(v.shape[:-1] + (-1, 32))
    amax = np.abs(blocks).max(-1, keepdims=True)
    byte = np.maximum(np.where(amax > 0, np.frexp(amax)[1] - 1 + 127, 0) - down, 1)
    scale = np.exp2(byte - 127.0)
    codes = (blocks / scale).astype(np.float32).astype(dtype).astype(np.float64)
    return np.moveaxis((codes * scale).reshape(v.shape), -1, axis)


WIDE = False


def mx_kscale(k):
    if not WIDE:
        return np.ones(k)
    levels = np.array([10, -10, 5, -5, 0])
    if k % 512:
        return np.exp2(np.random.permutation(np.resize(levels, k // 32))).repeat(32)
    a = np.empty((k // 512, 16))
    for p in range(k // 512):
        a[p, :8] = np.random.permutation(np.resize(levels, 8))
        for g in range(8):
            far = levels[np.abs(levels - a[p, g]) >= 10]
            a[p, g + 8] = far[np.random.randint(len(far))]
    return np.exp2(a.ravel()).repeat(32)


BF16 = ml_dtypes.bfloat16


def bf(x):
    return np.asarray(x, np.float32).astype(BF16)


def f64(x):
    return np.asarray(x).astype(np.float64)


B, S, D, E, R = 4, 2048, 1024, 8, 32


def setup_inputs():
    s = mx_kscale(D)
    return {"x": bf(np.random.standard_normal((B, S, D)) * s),
            "W": bf(np.random.standard_normal((E, R, D)) * (1.0 / np.sqrt(D)) / s)}


def reference(x, W):
    xq = mxq(f64(x), 2, "e4m3")
    Wq = mxq(f64(W), 2, "e4m3")
    y = xq[None, :, :, :] @ Wq.transpose(0, 2, 1)[:, None, :, :]
    return tuple(y[e] for e in range(W.shape[0]))

@@ -1,0 +1,188 @@
+from contextlib import ExitStack
+
+import concourse.mybir as mybir
+from concourse.masks import make_identity
+
+F32 = mybir.dt.float32
+BF16 = mybir.dt.bfloat16
+U32 = mybir.dt.uint32
+U8 = mybir.dt.uint8
+FP8X4 = mybir.dt.float8_e4m3fn_x4
+
+P = 128
+D = 1024
+ROWS = 8192
+E = 8
+R = 32
+COLS = E * R
+NT = ROWS // P
+WORDS = D // 2
+UNIT = 4
+
+FLOPS = 2 * ROWS * D * COLS
+
+GROUPS = (32, 16, 8, 8)
+CHUNKS = (1, 1, 2, 4, 4, 4, 4, 4, 4, 4, 8, 8, 8, 4, 4)
+CHUNK_BUFS = {1: 2, 2: 1, 4: 5, 8: 3}
+RUNS = (2, 2, 4, 8, 8, 8, 8, 8, 8, 4, 2, 2)
+
+
+def tile_moelineara_t_kernel(tc, x, W, *outs):
+    nc = tc.nc
+    xf = x.flatten_outer_dims()
+    wf = W.flatten_outer_dims()
+    of = [o.flatten_outer_dims() for o in outs]
+
+    group_of = []
+    first = 0
+    for s, t_count in enumerate(GROUPS):
+        group_of.extend([(s, first, t_count)] * t_count)
+        first += t_count
+    assert first == NT
+    chunk_first = []
+    first = 0
+    for cnt in CHUNKS:
+        chunk_first.append(first)
+        first += cnt
+    assert first == NT
+    run_first = []
+    first = 0
+    for cnt in RUNS:
+        run_first.append(first)
+        first += cnt
+    assert first == NT
+
+    with ExitStack() as ctx:
+        const = ctx.enter_context(tc.tile_pool(name="const", bufs=1))
+        xpool = ctx.enter_context(tc.tile_pool(name="xpool", bufs=1))
+        gpool = ctx.enter_context(tc.tile_pool(name="gpool", bufs=3))
+        qpool = ctx.enter_context(tc.tile_pool(name="qpool", bufs=4))
+        opool = ctx.enter_context(tc.tile_pool(name="opool", bufs=1))
+        psum_t = ctx.enter_context(tc.psum_pool(name="psum_t", bufs=4))
+        psum_o = ctx.enter_context(tc.psum_pool(name="psum_o", bufs=4))
+        ctx.enter_context(tc.manual_schedule())
+
+        tile_src = {}
+        holders = {}
+        state = {"chunk": 0, "transposed": 0}
+
+        def load_chunks():
+            while state["chunk"] < len(CHUNKS):
+                c = state["chunk"]
+                cnt = CHUNKS[c]
+                held = holders.get(cnt, [])
+                if len(held) >= CHUNK_BUFS[cnt]:
+                    old = held[len(held) - CHUNK_BUFS[cnt]]
+                    if chunk_first[old] + cnt > state["transposed"]:
+                        return
+                holders[cnt] = held + [c]
+                state["chunk"] = c + 1
+                n0 = chunk_first[c]
+                s, g0, t_count = group_of[n0]
+                xc = xpool.tile([P, cnt * D], BF16, name="x%d" % cnt, tag="x%d" % cnt, bufs=CHUNK_BUFS[cnt])
+                rows = xf[g0 * P:(g0 + t_count) * P, :].rearrange("(p t) k -> p t k", t=t_count)
+                nc.sync.dma_start(
+                    out=xc[:].rearrange("p (t k) -> p t k", k=D),
+                    in_=rows[:, n0 - g0:n0 - g0 + cnt, :],
+                )
+                xw = xc[:].bitcast(F32)
+                for j in range(cnt):
+                    tile_src[n0 + j] = (xw, j * WORDS)
+
+        def transpose_tile(words_ap, first_word):
+            xt = psum_t.tile([P, 4 * P], F32, name="xt")
+            for b in range(4):
+                first = first_word + (b // 2) * 2 * P + b % 2
+                nc.tensor.transpose(
+                    xt[:, b * P:(b + 1) * P],
+                    words_ap[:, first:first_word + (b // 2 + 1) * 2 * P:2],
+                    ident[:],
+                )
+            return xt[:].rearrange("p (g u r) -> p g r u", g=2, u=2)
+
+        def copy_on(k, out, in_):
+            if k % 2 == 0:
+                nc.vector.tensor_copy(out=out, in_=in_)
+            else:
+                nc.scalar.copy(out=out, in_=in_)
+
+        w_raw = const.tile([P, 2 * D], BF16, name="w_raw")
+        nc.sync.dma_start(
+            out=w_raw[:].rearrange("p (h k) -> p h k", h=2),
+            in_=wf.rearrange("(h p) k -> p h k", p=P),
+        )
+        load_chunks()
+
+        ident = const.tile([P, P], F32, name="ident")
+        make_identity(nc, ident[:])
+
+        w_grouped = const.tile([P, 2 * COLS * 4], BF16, name="w_grouped", align_bytes=64)
+        w_words = const.tile([P, 2 * COLS], U32, name="w_words", align_bytes=64)
+        w_scales = const.tile([P, 2 * COLS], U8, name="w_scales", align_bytes=64)
+        wg = w_grouped[:].bitcast(F32).rearrange("p (g c u) -> p g c u", g=2, u=2)
+        for h in range(2):
+            copy_on(h, wg[:, :, h * P:(h + 1) * P, :], transpose_tile(w_raw[:].bitcast(F32), h * WORDS))
+        nc.vector.quantize_mx(out=w_words[:].bitcast(FP8X4), scales=w_scales[:], in_=w_grouped[:])
+
+        quant = {}
+        out_sb = {}
+
+        def transpose_run(i):
+            n0 = run_first[i]
+            units = []
+            for u0 in range(n0, n0 + RUNS[i], UNIT):
+                cnt = min(UNIT, n0 + RUNS[i] - u0)
+                gt = gpool.tile([P, cnt * D], BF16, name="grouped", align_bytes=64)
+                gf = gt[:].bitcast(F32)
+                for j in range(cnt):
+                    xw, off = tile_src[u0 + j]
+                    copy_on(
+                        u0 + j,
+                        gf[:, j * WORDS:(j + 1) * WORDS].rearrange("p (g r u) -> p g r u", g=2, u=2),
+                        transpose_tile(xw, off),
+                    )
+                units.append((u0, cnt, gt))
+            state["transposed"] = n0 + RUNS[i]
+            load_chunks()
+            for u0, cnt, gt in units:
+                words = qpool.tile([P, cnt * 2 * P], U32, name="words", align_bytes=64)
+                scales = qpool.tile([P, cnt * 2 * P], U8, name="scales", align_bytes=64)
+                nc.vector.quantize_mx(out=words[:].bitcast(FP8X4), scales=scales[:], in_=gt[:])
+                for j in range(cnt):
+                    quant[u0 + j] = (words, scales, j * 2 * P)
+
+        def multiply_run(i):
+            for n in range(run_first[i], run_first[i] + RUNS[i], 2):
+                acc = psum_o.tile([P, 2 * COLS], F32, name="acc")
+                for jj in range(2):
+                    words, scales, c0 = quant[n + jj]
+                    for g in range(2):
+                        nc.tensor.matmul_mx(
+                            out=acc[:, jj * COLS:(jj + 1) * COLS],
+                            lhsT=words[:, c0 + g * P:c0 + (g + 1) * P].bitcast(FP8X4),
+                            lhsT_scale=scales[:, c0 + g * P:c0 + (g + 1) * P],
+                            rhs=w_words[:, g * COLS:(g + 1) * COLS].bitcast(FP8X4),
+                            rhs_scale=w_scales[:, g * COLS:(g + 1) * COLS],
+                            start=(g == 0),
+                            stop=(g == 1),
+                        )
+                s, g0, t_count = group_of[n]
+                if n == g0:
+                    out_sb[s] = opool.tile([P, E * t_count * R], F32, name="out%d" % s, tag="out%d" % s)
+                ov = out_sb[s][:].rearrange("p (e t r) -> p e t r", e=E, r=R)
+                nc.scalar.copy(
+                    out=ov[:, :, n - g0:n - g0 + 2, :],
+                    in_=acc[:].rearrange("p (t e r) -> p e t r", t=2, r=R),
+                )
+                if n + 2 == g0 + t_count:
+                    for e in range(E):
+                        nc.sync.dma_start(
+                            out=of[e][g0 * P:(g0 + t_count) * P, :].rearrange("(p t) r -> p t r", t=t_count),
+                            in_=ov[:, e, :, :],
+                        )
+
+        for i in range(len(RUNS) + 1):
+            if i < len(RUNS):
+                transpose_run(i)
+            if i >= 1:
+                multiply_run(i - 1)

@@ -17,14 +17,25 @@ R = 32
 COLS = E * R
 NT = ROWS // P
 WORDS = D // 2
-UNIT = 4
 
 FLOPS = 2 * ROWS * D * COLS
 
 GROUPS = (32, 16, 8, 8)
-CHUNKS = (1, 1, 2, 4, 4, 4, 4, 4, 4, 4, 8, 8, 8, 4, 4)
-CHUNK_BUFS = {1: 2, 2: 1, 4: 5, 8: 3}
-RUNS = (2, 2, 4, 8, 8, 8, 8, 8, 8, 4, 2, 2)
+CHUNKS = (1, 1, 2) + (4,) * 7 + (8,) * 4
+CHUNK_BUFS = {1: 2, 2: 1, 4: 4, 8: 4}
+UNITS = (2, 2) + (4,) * 15
+SORTED = (0, 0, 0) + (3, 4) * 7
+ON_VECTOR = (1, 1) + (1,) * 15
+
+
+def starts(counts):
+    out = []
+    first = 0
+    for cnt in counts:
+        out.append(first)
+        first += cnt
+    assert first == NT
+    return out
 
 
 def tile_moelineara_t_kernel(tc, x, W, *outs):
@@ -34,29 +45,17 @@ def tile_moelineara_t_kernel(tc, x, W, *outs):
     of = [o.flatten_outer_dims() for o in outs]
 
     group_of = []
-    first = 0
-    for s, t_count in enumerate(GROUPS):
+    for s, (first, t_count) in enumerate(zip(starts(GROUPS), GROUPS)):
         group_of.extend([(s, first, t_count)] * t_count)
-        first += t_count
-    assert first == NT
-    chunk_first = []
-    first = 0
-    for cnt in CHUNKS:
-        chunk_first.append(first)
-        first += cnt
-    assert first == NT
-    run_first = []
-    first = 0
-    for cnt in RUNS:
-        run_first.append(first)
-        first += cnt
-    assert first == NT
+    chunk_first = starts(CHUNKS)
+    unit_first = starts(UNITS)
 
     with ExitStack() as ctx:
         const = ctx.enter_context(tc.tile_pool(name="const", bufs=1))
         xpool = ctx.enter_context(tc.tile_pool(name="xpool", bufs=1))
-        gpool = ctx.enter_context(tc.tile_pool(name="gpool", bufs=3))
-        qpool = ctx.enter_context(tc.tile_pool(name="qpool", bufs=4))
+        rpool = ctx.enter_context(tc.tile_pool(name="rpool", bufs=3))
+        gpool = ctx.enter_context(tc.tile_pool(name="gpool", bufs=2))
+        qpool = ctx.enter_context(tc.tile_pool(name="qpool", bufs=3))
         opool = ctx.enter_context(tc.tile_pool(name="opool", bufs=1))
         psum_t = ctx.enter_context(tc.psum_pool(name="psum_t", bufs=4))
         psum_o = ctx.enter_context(tc.psum_pool(name="psum_o", bufs=4))
@@ -64,7 +63,7 @@ def tile_moelineara_t_kernel(tc, x, W, *outs):
 
         tile_src = {}
         holders = {}
-        state = {"chunk": 0, "transposed": 0}
+        state = {"chunk": 0, "sorted": 0}
 
         def load_chunks():
             while state["chunk"] < len(CHUNKS):
@@ -73,7 +72,7 @@ def tile_moelineara_t_kernel(tc, x, W, *outs):
                 held = holders.get(cnt, [])
                 if len(held) >= CHUNK_BUFS[cnt]:
                     old = held[len(held) - CHUNK_BUFS[cnt]]
-                    if chunk_first[old] + cnt > state["transposed"]:
+                    if chunk_first[old] + cnt > state["sorted"]:
                         return
                 holders[cnt] = held + [c]
                 state["chunk"] = c + 1
@@ -89,22 +88,101 @@ def tile_moelineara_t_kernel(tc, x, W, *outs):
                 for j in range(cnt):
                     tile_src[n0 + j] = (xw, j * WORDS)
 
-        def transpose_tile(words_ap, first_word):
+        def transpose_tile(words_ap, first_word, is_sorted):
             xt = psum_t.tile([P, 4 * P], F32, name="xt")
-            for b in range(4):
-                first = first_word + (b // 2) * 2 * P + b % 2
-                nc.tensor.transpose(
-                    xt[:, b * P:(b + 1) * P],
-                    words_ap[:, first:first_word + (b // 2 + 1) * 2 * P:2],
-                    ident[:],
-                )
+            for g in range(2):
+                for u in range(2):
+                    first = first_word + 2 * g * P
+                    if is_sorted:
+                        cols = slice(first + u * P, first + (u + 1) * P)
+                    else:
+                        cols = slice(first + u, first + 2 * P, 2)
+                    nc.tensor.transpose(xt[:, (2 * g + u) * P:(2 * g + u + 1) * P], words_ap[:, cols], ident[:])
             return xt[:].rearrange("p (g u r) -> p g r u", g=2, u=2)
 
-        def copy_on(k, out, in_):
-            if k % 2 == 0:
-                nc.vector.tensor_copy(out=out, in_=in_)
-            else:
-                nc.scalar.copy(out=out, in_=in_)
+        sorted_words = {}
+
+        def sort_unit(i):
+            n0, cnt, sorted_cnt = unit_first[i], UNITS[i], SORTED[i]
+            if sorted_cnt == 0:
+                return
+            xs = rpool.tile([P, sorted_cnt * D], BF16, name="xs")
+            xsf = xs[:].bitcast(F32)
+            xw, off = tile_src[n0 + cnt - sorted_cnt]
+            nc.vector.tensor_copy(
+                out=xsf.rearrange("p (b u w) -> p b u w", u=2, w=P),
+                in_=xw[:, off:off + sorted_cnt * WORDS].rearrange("p (b w u) -> p b u w", u=2, w=P),
+            )
+            for j in range(sorted_cnt):
+                sorted_words[n0 + cnt - sorted_cnt + j] = (xsf, j * WORDS)
+            if sorted_cnt == cnt:
+                state["sorted"] = n0 + cnt
+                load_chunks()
+
+        grouped = {}
+
+        def transpose_unit(i):
+            n0, cnt = unit_first[i], UNITS[i]
+            gt = gpool.tile([P, cnt * D], BF16, name="gt", align_bytes=64)
+            gf = gt[:].bitcast(F32)
+            for j in range(cnt):
+                is_sorted = n0 + j in sorted_words
+                xw, off = sorted_words[n0 + j] if is_sorted else tile_src[n0 + j]
+                src = transpose_tile(xw, off, is_sorted)
+                dst = gf[:, j * WORDS:(j + 1) * WORDS].rearrange("p (g r u) -> p g r u", g=2, u=2)
+                if j >= cnt - ON_VECTOR[i]:
+                    nc.vector.tensor_copy(out=dst, in_=src)
+                else:
+                    nc.scalar.copy(out=dst, in_=src)
+            grouped[i] = gt
+            if SORTED[i] < cnt:
+                state["sorted"] = max(state["sorted"], n0 + cnt)
+                load_chunks()
+
+        quant = {}
+
+        def quantise_unit(i):
+            cnt = UNITS[i]
+            words = qpool.tile([P, cnt * 2 * P], U32, name="words", align_bytes=64)
+            scales = qpool.tile([P, cnt * 2 * P], U8, name="scales", align_bytes=64)
+            nc.vector.quantize_mx(out=words[:].bitcast(FP8X4), scales=scales[:], in_=grouped[i][:])
+            quant[i] = (words, scales)
+
+        out_sb = {}
+
+        def multiply_unit(i):
+            words, scales = quant[i]
+            n0, cnt = unit_first[i], UNITS[i]
+            for j0 in range(0, cnt, 2):
+                pair = min(2, cnt - j0)
+                acc = psum_o.tile([P, 2 * COLS], F32, name="acc")
+                for jj in range(pair):
+                    c0 = (j0 + jj) * 2 * P
+                    for g in range(2):
+                        nc.tensor.matmul_mx(
+                            out=acc[:, jj * COLS:(jj + 1) * COLS],
+                            lhsT=words[:, c0 + g * P:c0 + (g + 1) * P].bitcast(FP8X4),
+                            lhsT_scale=scales[:, c0 + g * P:c0 + (g + 1) * P],
+                            rhs=w_words[:, g * COLS:(g + 1) * COLS].bitcast(FP8X4),
+                            rhs_scale=w_scales[:, g * COLS:(g + 1) * COLS],
+                            start=(g == 0),
+                            stop=(g == 1),
+                        )
+                n = n0 + j0
+                s, g0, t_count = group_of[n]
+                if n == g0:
+                    out_sb[s] = opool.tile([P, E * t_count * R], F32, name="out%d" % s, tag="out%d" % s)
+                ov = out_sb[s][:].rearrange("p (e t r) -> p e t r", e=E, r=R)
+                nc.scalar.copy(
+                    out=ov[:, :, n - g0:n - g0 + pair, :],
+                    in_=acc[:, 0:pair * COLS].rearrange("p (t e r) -> p e t r", t=pair, r=R),
+                )
+                if n + pair == g0 + t_count:
+                    for e in range(E):
+                        nc.sync.dma_start(
+                            out=of[e][g0 * P:(g0 + t_count) * P, :].rearrange("(p t) r -> p t r", t=t_count),
+                            in_=ov[:, e, :, :],
+                        )
 
         w_raw = const.tile([P, 2 * D], BF16, name="w_raw")
         nc.sync.dma_start(
@@ -120,69 +198,17 @@ def tile_moelineara_t_kernel(tc, x, W, *outs):
         w_words = const.tile([P, 2 * COLS], U32, name="w_words", align_bytes=64)
         w_scales = const.tile([P, 2 * COLS], U8, name="w_scales", align_bytes=64)
         wg = w_grouped[:].bitcast(F32).rearrange("p (g c u) -> p g c u", g=2, u=2)
-        for h in range(2):
-            copy_on(h, wg[:, :, h * P:(h + 1) * P, :], transpose_tile(w_raw[:].bitcast(F32), h * WORDS))
+        w_raw_words = w_raw[:].bitcast(F32)
+        nc.scalar.copy(out=wg[:, :, 0:P, :], in_=transpose_tile(w_raw_words, 0, False))
+        nc.vector.tensor_copy(out=wg[:, :, P:2 * P, :], in_=transpose_tile(w_raw_words, WORDS, False))
         nc.vector.quantize_mx(out=w_words[:].bitcast(FP8X4), scales=w_scales[:], in_=w_grouped[:])
 
-        quant = {}
-        out_sb = {}
-
-        def transpose_run(i):
-            n0 = run_first[i]
-            units = []
-            for u0 in range(n0, n0 + RUNS[i], UNIT):
-                cnt = min(UNIT, n0 + RUNS[i] - u0)
-                gt = gpool.tile([P, cnt * D], BF16, name="grouped", align_bytes=64)
-                gf = gt[:].bitcast(F32)
-                for j in range(cnt):
-                    xw, off = tile_src[u0 + j]
-                    copy_on(
-                        u0 + j,
-                        gf[:, j * WORDS:(j + 1) * WORDS].rearrange("p (g r u) -> p g r u", g=2, u=2),
-                        transpose_tile(xw, off),
-                    )
-                units.append((u0, cnt, gt))
-            state["transposed"] = n0 + RUNS[i]
-            load_chunks()
-            for u0, cnt, gt in units:
-                words = qpool.tile([P, cnt * 2 * P], U32, name="words", align_bytes=64)
-                scales = qpool.tile([P, cnt * 2 * P], U8, name="scales", align_bytes=64)
-                nc.vector.quantize_mx(out=words[:].bitcast(FP8X4), scales=scales[:], in_=gt[:])
-                for j in range(cnt):
-                    quant[u0 + j] = (words, scales, j * 2 * P)
-
-        def multiply_run(i):
-            for n in range(run_first[i], run_first[i] + RUNS[i], 2):
-                acc = psum_o.tile([P, 2 * COLS], F32, name="acc")
-                for jj in range(2):
-                    words, scales, c0 = quant[n + jj]
-                    for g in range(2):
-                        nc.tensor.matmul_mx(
-                            out=acc[:, jj * COLS:(jj + 1) * COLS],
-                            lhsT=words[:, c0 + g * P:c0 + (g + 1) * P].bitcast(FP8X4),
-                            lhsT_scale=scales[:, c0 + g * P:c0 + (g + 1) * P],
-                            rhs=w_words[:, g * COLS:(g + 1) * COLS].bitcast(FP8X4),
-                            rhs_scale=w_scales[:, g * COLS:(g + 1) * COLS],
-                            start=(g == 0),
-                            stop=(g == 1),
-                        )
-                s, g0, t_count = group_of[n]
-                if n == g0:
-                    out_sb[s] = opool.tile([P, E * t_count * R], F32, name="out%d" % s, tag="out%d" % s)
-                ov = out_sb[s][:].rearrange("p (e t r) -> p e t r", e=E, r=R)
-                nc.scalar.copy(
-                    out=ov[:, :, n - g0:n - g0 + 2, :],
-                    in_=acc[:].rearrange("p (t e r) -> p e t r", t=2, r=R),
-                )
-                if n + 2 == g0 + t_count:
-                    for e in range(E):
-                        nc.sync.dma_start(
-                            out=of[e][g0 * P:(g0 + t_count) * P, :].rearrange("(p t) r -> p t r", t=t_count),
-                            in_=ov[:, e, :, :],
-                        )
-
-        for i in range(len(RUNS) + 1):
-            if i < len(RUNS):
-                transpose_run(i)
-            if i >= 1:
-                multiply_run(i - 1)
+        for i in range(len(UNITS) + 2):
+            if i + 1 < len(UNITS):
+                sort_unit(i + 1)
+            if i >= 1 and i - 1 < len(UNITS):
+                quantise_unit(i - 1)
+            if i < len(UNITS):
+                transpose_unit(i)
+            if i >= 2:
+                multiply_unit(i - 2)

@@ -21,11 +21,12 @@ WORDS = D // 2
 FLOPS = 2 * ROWS * D * COLS
 
 GROUPS = (32, 16, 8, 8)
-CHUNKS = (1, 1, 2) + (4,) * 7 + (8,) * 4
-CHUNK_BUFS = {1: 2, 2: 1, 4: 4, 8: 4}
-UNITS = (2, 2) + (4,) * 15
-SORTED = (0, 0, 0) + (3, 4) * 7
-ON_VECTOR = (1, 1) + (1,) * 15
+CHUNKS = (1, 1, 2, 2, 2) + (4,) * 6 + (8,) * 4
+CHUNK_BUFS = {1: 2, 2: 3, 4: 4, 8: 4}
+UNITS = (2, 2, 2, 2) + (4,) * 13 + (2, 2)
+SORTED = (0, 0, 0, 0, 4) + (4,) * 12 + (2, 2)
+W_AFTER = 0
+ON_VECTOR = (1,) * 19
 
 
 def starts(counts):
@@ -53,12 +54,12 @@ def tile_moelineara_t_kernel(tc, x, W, *outs):
     with ExitStack() as ctx:
         const = ctx.enter_context(tc.tile_pool(name="const", bufs=1))
         xpool = ctx.enter_context(tc.tile_pool(name="xpool", bufs=1))
-        rpool = ctx.enter_context(tc.tile_pool(name="rpool", bufs=3))
+        rpool = ctx.enter_context(tc.tile_pool(name="rpool", bufs=2))
         gpool = ctx.enter_context(tc.tile_pool(name="gpool", bufs=2))
         qpool = ctx.enter_context(tc.tile_pool(name="qpool", bufs=3))
         opool = ctx.enter_context(tc.tile_pool(name="opool", bufs=1))
-        psum_t = ctx.enter_context(tc.psum_pool(name="psum_t", bufs=4))
-        psum_o = ctx.enter_context(tc.psum_pool(name="psum_o", bufs=4))
+        psum_t = ctx.enter_context(tc.psum_pool(name="psum_t", bufs=5))
+        psum_o = ctx.enter_context(tc.psum_pool(name="psum_o", bufs=3))
         ctx.enter_context(tc.manual_schedule())
 
         tile_src = {}
@@ -68,6 +69,11 @@ def tile_moelineara_t_kernel(tc, x, W, *outs):
         def load_chunks():
             while state["chunk"] < len(CHUNKS):
                 c = state["chunk"]
+                if c == W_AFTER:
+                    nc.sync.dma_start(
+                        out=w_raw[:].rearrange("p (h k) -> p h k", h=2),
+                        in_=wf.rearrange("(h p) k -> p h k", p=P),
+                    )
                 cnt = CHUNKS[c]
                 held = holders.get(cnt, [])
                 if len(held) >= CHUNK_BUFS[cnt]:
@@ -145,7 +151,12 @@ def tile_moelineara_t_kernel(tc, x, W, *outs):
             cnt = UNITS[i]
             words = qpool.tile([P, cnt * 2 * P], U32, name="words", align_bytes=64)
             scales = qpool.tile([P, cnt * 2 * P], U8, name="scales", align_bytes=64)
-            nc.vector.quantize_mx(out=words[:].bitcast(FP8X4), scales=scales[:], in_=grouped[i][:])
+            for j0 in range(0, cnt, 4):
+                j1 = min(cnt, j0 + 4)
+                cols = slice(j0 * 2 * P, j1 * 2 * P)
+                nc.vector.quantize_mx(
+                    out=words[:, cols].bitcast(FP8X4), scales=scales[:, cols], in_=grouped[i][:, j0 * D:j1 * D]
+                )
             quant[i] = (words, scales)
 
         out_sb = {}
@@ -185,30 +196,36 @@ def tile_moelineara_t_kernel(tc, x, W, *outs):
                         )
 
         w_raw = const.tile([P, 2 * D], BF16, name="w_raw")
-        nc.sync.dma_start(
-            out=w_raw[:].rearrange("p (h k) -> p h k", h=2),
-            in_=wf.rearrange("(h p) k -> p h k", p=P),
-        )
         load_chunks()
 
         ident = const.tile([P, P], F32, name="ident")
         make_identity(nc, ident[:])
 
+        def prepare_weights():
+            w_raw_words = w_raw[:].bitcast(F32)
+            wg = w_grouped[:].bitcast(F32).rearrange("p (g c u) -> p g c u", g=2, u=2)
+            nc.scalar.copy(out=wg[:, :, 0:P, :], in_=transpose_tile(w_raw_words, 0, False))
+            nc.vector.tensor_copy(out=wg[:, :, P:2 * P, :], in_=transpose_tile(w_raw_words, WORDS, False))
+
+        def quantise_weights():
+            nc.vector.quantize_mx(out=w_words[:].bitcast(FP8X4), scales=w_scales[:], in_=w_grouped[:])
+
         w_grouped = const.tile([P, 2 * COLS * 4], BF16, name="w_grouped", align_bytes=64)
         w_words = const.tile([P, 2 * COLS], U32, name="w_words", align_bytes=64)
         w_scales = const.tile([P, 2 * COLS], U8, name="w_scales", align_bytes=64)
-        wg = w_grouped[:].bitcast(F32).rearrange("p (g c u) -> p g c u", g=2, u=2)
-        w_raw_words = w_raw[:].bitcast(F32)
-        nc.scalar.copy(out=wg[:, :, 0:P, :], in_=transpose_tile(w_raw_words, 0, False))
-        nc.vector.tensor_copy(out=wg[:, :, P:2 * P, :], in_=transpose_tile(w_raw_words, WORDS, False))
-        nc.vector.quantize_mx(out=w_words[:].bitcast(FP8X4), scales=w_scales[:], in_=w_grouped[:])
-
-        for i in range(len(UNITS) + 2):
-            if i + 1 < len(UNITS):
+        prepare_weights()
+        quantise_weights()
+        sort_unit(0)
+        last = len(UNITS) - 1
+        multiplied = 0
+        for i in range(last + 2):
+            if i < last:
                 sort_unit(i + 1)
-            if i >= 1 and i - 1 < len(UNITS):
+            if i >= 1:
                 quantise_unit(i - 1)
-            if i < len(UNITS):
+            if i <= last:
                 transpose_unit(i)
-            if i >= 2:
-                multiply_unit(i - 2)
+            behind = 2 if i < last else 1
+            while multiplied <= i - behind:
+                multiply_unit(multiplied)
+                multiplied += 1

@@ -24,7 +24,8 @@ GROUPS = (32, 16, 8, 8)
 CHUNKS = (1, 1, 2, 2, 2) + (4,) * 6 + (8,) * 4
 CHUNK_BUFS = {1: 2, 2: 3, 4: 4, 8: 4}
 UNITS = (2, 2, 2, 2) + (4,) * 13 + (2, 2)
-SORTED = (0, 0, 0, 0, 4) + (4,) * 12 + (2, 2)
+RUN = 4
+SORTED = (0, 0, 0, 0, 3) + (3,) * 12 + (2, 0)
 W_AFTER = 0
 ON_VECTOR = (1,) * 19
 
@@ -94,15 +95,16 @@ def tile_moelineara_t_kernel(tc, x, W, *outs):
                 for j in range(cnt):
                     tile_src[n0 + j] = (xw, j * WORDS)
 
-        def transpose_tile(words_ap, first_word, is_sorted):
+        def transpose_tile(words_ap, first_word, odd):
             xt = psum_t.tile([P, 4 * P], F32, name="xt")
             for g in range(2):
                 for u in range(2):
-                    first = first_word + 2 * g * P
-                    if is_sorted:
-                        cols = slice(first + u * P, first + (u + 1) * P)
-                    else:
+                    if odd == 1:
+                        first = first_word + 2 * g * P
                         cols = slice(first + u, first + 2 * P, 2)
+                    else:
+                        first = first_word + u * odd + g * P
+                        cols = slice(first, first + P)
                     nc.tensor.transpose(xt[:, (2 * g + u) * P:(2 * g + u + 1) * P], words_ap[:, cols], ident[:])
             return xt[:].rearrange("p (g u r) -> p g r u", g=2, u=2)
 
@@ -116,11 +118,11 @@ def tile_moelineara_t_kernel(tc, x, W, *outs):
             xsf = xs[:].bitcast(F32)
             xw, off = tile_src[n0 + cnt - sorted_cnt]
             nc.vector.tensor_copy(
-                out=xsf.rearrange("p (b u w) -> p b u w", u=2, w=P),
-                in_=xw[:, off:off + sorted_cnt * WORDS].rearrange("p (b w u) -> p b u w", u=2, w=P),
+                out=xsf.rearrange("p (u n w) -> p n u w", u=2, w=RUN),
+                in_=xw[:, off:off + sorted_cnt * WORDS].rearrange("p (n w u) -> p n u w", u=2, w=RUN),
             )
             for j in range(sorted_cnt):
-                sorted_words[n0 + cnt - sorted_cnt + j] = (xsf, j * WORDS)
+                sorted_words[n0 + cnt - sorted_cnt + j] = (xsf, j * 2 * P, sorted_cnt * 2 * P)
             if sorted_cnt == cnt:
                 state["sorted"] = n0 + cnt
                 load_chunks()
@@ -132,9 +134,8 @@ def tile_moelineara_t_kernel(tc, x, W, *outs):
             gt = gpool.tile([P, cnt * D], BF16, name="gt", align_bytes=64)
             gf = gt[:].bitcast(F32)
             for j in range(cnt):
-                is_sorted = n0 + j in sorted_words
-                xw, off = sorted_words[n0 + j] if is_sorted else tile_src[n0 + j]
-                src = transpose_tile(xw, off, is_sorted)
+                xw, off, odd = sorted_words.get(n0 + j, tile_src[n0 + j] + (1,))
+                src = transpose_tile(xw, off, odd)
                 dst = gf[:, j * WORDS:(j + 1) * WORDS].rearrange("p (g r u) -> p g r u", g=2, u=2)
                 if j >= cnt - ON_VECTOR[i]:
                     nc.vector.tensor_copy(out=dst, in_=src)
@@ -204,8 +205,8 @@ def tile_moelineara_t_kernel(tc, x, W, *outs):
         def prepare_weights():
             w_raw_words = w_raw[:].bitcast(F32)
             wg = w_grouped[:].bitcast(F32).rearrange("p (g c u) -> p g c u", g=2, u=2)
-            nc.scalar.copy(out=wg[:, :, 0:P, :], in_=transpose_tile(w_raw_words, 0, False))
-            nc.vector.tensor_copy(out=wg[:, :, P:2 * P, :], in_=transpose_tile(w_raw_words, WORDS, False))
+            nc.scalar.copy(out=wg[:, :, 0:P, :], in_=transpose_tile(w_raw_words, 0, 1))
+            nc.vector.tensor_copy(out=wg[:, :, P:2 * P, :], in_=transpose_tile(w_raw_words, WORDS, 1))
 
         def quantise_weights():
             nc.vector.quantize_mx(out=w_words[:].bitcast(FP8X4), scales=w_scales[:], in_=w_grouped[:])

@@ -21,13 +21,11 @@ WORDS = D // 2
 FLOPS = 2 * ROWS * D * COLS
 
 GROUPS = (32, 16, 8, 8)
-CHUNKS = (1, 1, 2, 2, 2) + (4,) * 6 + (8,) * 4
-CHUNK_BUFS = {1: 2, 2: 3, 4: 4, 8: 4}
+CHUNKS = (2, 2, 2, 2) + (4,) * 6 + (8,) * 4
+CHUNK_BUFS = {2: 4, 4: 4, 8: 4}
 UNITS = (2, 2, 2, 2) + (4,) * 13 + (2, 2)
 RUN = 4
 SORTED = (0, 0, 0, 0, 3) + (3,) * 12 + (2, 0)
-W_AFTER = 0
-ON_VECTOR = (1,) * 19
 
 
 def starts(counts):
@@ -51,6 +49,7 @@ def tile_moelineara_t_kernel(tc, x, W, *outs):
         group_of.extend([(s, first, t_count)] * t_count)
     chunk_first = starts(CHUNKS)
     unit_first = starts(UNITS)
+    last = len(UNITS) - 1
 
     with ExitStack() as ctx:
         const = ctx.enter_context(tc.tile_pool(name="const", bufs=1))
@@ -70,11 +69,6 @@ def tile_moelineara_t_kernel(tc, x, W, *outs):
         def load_chunks():
             while state["chunk"] < len(CHUNKS):
                 c = state["chunk"]
-                if c == W_AFTER:
-                    nc.sync.dma_start(
-                        out=w_raw[:].rearrange("p (h k) -> p h k", h=2),
-                        in_=wf.rearrange("(h p) k -> p h k", p=P),
-                    )
                 cnt = CHUNKS[c]
                 held = holders.get(cnt, [])
                 if len(held) >= CHUNK_BUFS[cnt]:
@@ -137,7 +131,7 @@ def tile_moelineara_t_kernel(tc, x, W, *outs):
                 xw, off, odd = sorted_words.get(n0 + j, tile_src[n0 + j] + (1,))
                 src = transpose_tile(xw, off, odd)
                 dst = gf[:, j * WORDS:(j + 1) * WORDS].rearrange("p (g r u) -> p g r u", g=2, u=2)
-                if j >= cnt - ON_VECTOR[i]:
+                if j == (0 if i == last else cnt - 1):
                     nc.vector.tensor_copy(out=dst, in_=src)
                 else:
                     nc.scalar.copy(out=dst, in_=src)
@@ -165,8 +159,9 @@ def tile_moelineara_t_kernel(tc, x, W, *outs):
         def multiply_unit(i):
             words, scales = quant[i]
             n0, cnt = unit_first[i], UNITS[i]
-            for j0 in range(0, cnt, 2):
-                pair = min(2, cnt - j0)
+            width = 1 if i == last else 2
+            for j0 in range(0, cnt, width):
+                pair = min(width, cnt - j0)
                 acc = psum_o.tile([P, 2 * COLS], F32, name="acc")
                 for jj in range(pair):
                     c0 = (j0 + jj) * 2 * P
@@ -185,10 +180,12 @@ def tile_moelineara_t_kernel(tc, x, W, *outs):
                 if n == g0:
                     out_sb[s] = opool.tile([P, E * t_count * R], F32, name="out%d" % s, tag="out%d" % s)
                 ov = out_sb[s][:].rearrange("p (e t r) -> p e t r", e=E, r=R)
-                nc.scalar.copy(
-                    out=ov[:, :, n - g0:n - g0 + pair, :],
-                    in_=acc[:, 0:pair * COLS].rearrange("p (t e r) -> p e t r", t=pair, r=R),
-                )
+                dst = ov[:, :, n - g0:n - g0 + pair, :]
+                src = acc[:, 0:pair * COLS].rearrange("p (t e r) -> p e t r", t=pair, r=R)
+                if i == last and j0 == 0:
+                    nc.vector.tensor_copy(out=dst, in_=src)
+                else:
+                    nc.scalar.copy(out=dst, in_=src)
                 if n + pair == g0 + t_count:
                     for e in range(E):
                         nc.sync.dma_start(
@@ -197,10 +194,24 @@ def tile_moelineara_t_kernel(tc, x, W, *outs):
                         )
 
         w_raw = const.tile([P, 2 * D], BF16, name="w_raw")
+        nc.sync.dma_start(
+            out=w_raw[:].rearrange("p (h k) -> p h k", h=2),
+            in_=wf.rearrange("(h p) k -> p h k", p=P),
+        )
         load_chunks()
 
         ident = const.tile([P, P], F32, name="ident")
         make_identity(nc, ident[:])
+
+        zeros = const.tile([P, 4 * P], BF16, name="zeros")
+        nc.vector.memset(zeros[:], 0.0)
+
+        def warm_up(count, columns):
+            spare = psum_o.tile([P, 2 * COLS], F32, name="acc")
+            for k in range(count):
+                nc.tensor.matmul(spare[:, 0:columns], zeros[:, 0:P], zeros[:, 0:columns], start=True, stop=True)
+
+        warm_up(5, 4 * P)
 
         def prepare_weights():
             w_raw_words = w_raw[:].bitcast(F32)
@@ -215,9 +226,9 @@ def tile_moelineara_t_kernel(tc, x, W, *outs):
         w_words = const.tile([P, 2 * COLS], U32, name="w_words", align_bytes=64)
         w_scales = const.tile([P, 2 * COLS], U8, name="w_scales", align_bytes=64)
         prepare_weights()
+        warm_up(1, 2 * P)
         quantise_weights()
         sort_unit(0)
-        last = len(UNITS) - 1
         multiplied = 0
         for i in range(last + 2):
             if i < last:
@@ -226,6 +237,8 @@ def tile_moelineara_t_kernel(tc, x, W, *outs):
                 quantise_unit(i - 1)
             if i <= last:
                 transpose_unit(i)
+            if i < 3:
+                warm_up(1, 2 * P)
             behind = 2 if i < last else 1
             while multiplied <= i - behind:
                 multiply_unit(multiplied)

@@ -203,16 +203,6 @@ def tile_moelineara_t_kernel(tc, x, W, *outs):
         ident = const.tile([P, P], F32, name="ident")
         make_identity(nc, ident[:])
 
-        zeros = const.tile([P, 4 * P], BF16, name="zeros")
-        nc.vector.memset(zeros[:], 0.0)
-
-        def warm_up(count, columns):
-            spare = psum_o.tile([P, 2 * COLS], F32, name="acc")
-            for k in range(count):
-                nc.tensor.matmul(spare[:, 0:columns], zeros[:, 0:P], zeros[:, 0:columns], start=True, stop=True)
-
-        warm_up(5, 4 * P)
-
         def prepare_weights():
             w_raw_words = w_raw[:].bitcast(F32)
             wg = w_grouped[:].bitcast(F32).rearrange("p (g c u) -> p g c u", g=2, u=2)
@@ -226,7 +216,6 @@ def tile_moelineara_t_kernel(tc, x, W, *outs):
         w_words = const.tile([P, 2 * COLS], U32, name="w_words", align_bytes=64)
         w_scales = const.tile([P, 2 * COLS], U8, name="w_scales", align_bytes=64)
         prepare_weights()
-        warm_up(1, 2 * P)
         quantise_weights()
         sort_unit(0)
         multiplied = 0
@@ -237,8 +226,6 @@ def tile_moelineara_t_kernel(tc, x, W, *outs):
                 quantise_unit(i - 1)
             if i <= last:
                 transpose_unit(i)
-            if i < 3:
-                warm_up(1, 2 * P)
             behind = 2 if i < last else 1
             while multiplied <= i - behind:
                 multiply_unit(multiplied)

from contextlib import ExitStack

import concourse.mybir as mybir
from concourse.masks import make_identity

F32 = mybir.dt.float32
BF16 = mybir.dt.bfloat16
U32 = mybir.dt.uint32
U8 = mybir.dt.uint8
FP8X4 = mybir.dt.float8_e4m3fn_x4

P = 128
D = 1024
ROWS = 8192
E = 8
R = 32
COLS = E * R
NT = ROWS // P
WORDS = D // 2

FLOPS = 2 * ROWS * D * COLS

GROUPS = (32, 16, 8, 8)
CHUNKS = (2, 2, 2, 2) + (4,) * 6 + (8,) * 4
CHUNK_BUFS = {2: 4, 4: 4, 8: 4}
UNITS = (2, 2, 2, 2) + (4,) * 13 + (2, 2)
RUN = 4
SORTED = (0, 0, 0, 0, 3) + (3,) * 12 + (2, 0)


def starts(counts):
    out = []
    first = 0
    for cnt in counts:
        out.append(first)
        first += cnt
    assert first == NT
    return out


def tile_moelineara_t_kernel(tc, x, W, *outs):
    nc = tc.nc
    xf = x.flatten_outer_dims()
    wf = W.flatten_outer_dims()
    of = [o.flatten_outer_dims() for o in outs]

    group_of = []
    for s, (first, t_count) in enumerate(zip(starts(GROUPS), GROUPS)):
        group_of.extend([(s, first, t_count)] * t_count)
    chunk_first = starts(CHUNKS)
    unit_first = starts(UNITS)
    last = len(UNITS) - 1

    with ExitStack() as ctx:
        const = ctx.enter_context(tc.tile_pool(name="const", bufs=1))
        xpool = ctx.enter_context(tc.tile_pool(name="xpool", bufs=1))
        rpool = ctx.enter_context(tc.tile_pool(name="rpool", bufs=2))
        gpool = ctx.enter_context(tc.tile_pool(name="gpool", bufs=2))
        qpool = ctx.enter_context(tc.tile_pool(name="qpool", bufs=3))
        opool = ctx.enter_context(tc.tile_pool(name="opool", bufs=1))
        psum_t = ctx.enter_context(tc.psum_pool(name="psum_t", bufs=5))
        psum_o = ctx.enter_context(tc.psum_pool(name="psum_o", bufs=3))
        ctx.enter_context(tc.manual_schedule())

        tile_src = {}
        holders = {}
        state = {"chunk": 0, "sorted": 0}

        def load_chunks():
            while state["chunk"] < len(CHUNKS):
                c = state["chunk"]
                cnt = CHUNKS[c]
                held = holders.get(cnt, [])
                if len(held) >= CHUNK_BUFS[cnt]:
                    old = held[len(held) - CHUNK_BUFS[cnt]]
                    if chunk_first[old] + cnt > state["sorted"]:
                        return
                holders[cnt] = held + [c]
                state["chunk"] = c + 1
                n0 = chunk_first[c]
                s, g0, t_count = group_of[n0]
                xc = xpool.tile([P, cnt * D], BF16, name="x%d" % cnt, tag="x%d" % cnt, bufs=CHUNK_BUFS[cnt])
                rows = xf[g0 * P:(g0 + t_count) * P, :].rearrange("(p t) k -> p t k", t=t_count)
                nc.sync.dma_start(
                    out=xc[:].rearrange("p (t k) -> p t k", k=D),
                    in_=rows[:, n0 - g0:n0 - g0 + cnt, :],
                )
                xw = xc[:].bitcast(F32)
                for j in range(cnt):
                    tile_src[n0 + j] = (xw, j * WORDS)

        def transpose_tile(words_ap, first_word, odd):
            xt = psum_t.tile([P, 4 * P], F32, name="xt")
            for g in range(2):
                for u in range(2):
                    if odd == 1:
                        first = first_word + 2 * g * P
                        cols = slice(first + u, first + 2 * P, 2)
                    else:
                        first = first_word + u * odd + g * P
                        cols = slice(first, first + P)
                    nc.tensor.transpose(xt[:, (2 * g + u) * P:(2 * g + u + 1) * P], words_ap[:, cols], ident[:])
            return xt[:].rearrange("p (g u r) -> p g r u", g=2, u=2)

        sorted_words = {}

        def sort_unit(i):
            n0, cnt, sorted_cnt = unit_first[i], UNITS[i], SORTED[i]
            if sorted_cnt == 0:
                return
            xs = rpool.tile([P, sorted_cnt * D], BF16, name="xs")
            xsf = xs[:].bitcast(F32)
            xw, off = tile_src[n0 + cnt - sorted_cnt]
            nc.vector.tensor_copy(
                out=xsf.rearrange("p (u n w) -> p n u w", u=2, w=RUN),
                in_=xw[:, off:off + sorted_cnt * WORDS].rearrange("p (n w u) -> p n u w", u=2, w=RUN),
            )
            for j in range(sorted_cnt):
                sorted_words[n0 + cnt - sorted_cnt + j] = (xsf, j * 2 * P, sorted_cnt * 2 * P)
            if sorted_cnt == cnt:
                state["sorted"] = n0 + cnt
                load_chunks()

        grouped = {}

        def transpose_unit(i):
            n0, cnt = unit_first[i], UNITS[i]
            gt = gpool.tile([P, cnt * D], BF16, name="gt", align_bytes=64)
            gf = gt[:].bitcast(F32)
            for j in range(cnt):
                xw, off, odd = sorted_words.get(n0 + j, tile_src[n0 + j] + (1,))
                src = transpose_tile(xw, off, odd)
                dst = gf[:, j * WORDS:(j + 1) * WORDS].rearrange("p (g r u) -> p g r u", g=2, u=2)
                if j == (0 if i == last else cnt - 1):
                    nc.vector.tensor_copy(out=dst, in_=src)
                else:
                    nc.scalar.copy(out=dst, in_=src)
            grouped[i] = gt
            if SORTED[i] < cnt:
                state["sorted"] = max(state["sorted"], n0 + cnt)
                load_chunks()

        quant = {}

        def quantise_unit(i):
            cnt = UNITS[i]
            words = qpool.tile([P, cnt * 2 * P], U32, name="words", align_bytes=64)
            scales = qpool.tile([P, cnt * 2 * P], U8, name="scales", align_bytes=64)
            for j0 in range(0, cnt, 4):
                j1 = min(cnt, j0 + 4)
                cols = slice(j0 * 2 * P, j1 * 2 * P)
                nc.vector.quantize_mx(
                    out=words[:, cols].bitcast(FP8X4), scales=scales[:, cols], in_=grouped[i][:, j0 * D:j1 * D]
                )
            quant[i] = (words, scales)

        out_sb = {}

        def multiply_unit(i):
            words, scales = quant[i]
            n0, cnt = unit_first[i], UNITS[i]
            width = 1 if i == last else 2
            for j0 in range(0, cnt, width):
                pair = min(width, cnt - j0)
                acc = psum_o.tile([P, 2 * COLS], F32, name="acc")
                for jj in range(pair):
                    c0 = (j0 + jj) * 2 * P
                    for g in range(2):
                        nc.tensor.matmul_mx(
                            out=acc[:, jj * COLS:(jj + 1) * COLS],
                            lhsT=words[:, c0 + g * P:c0 + (g + 1) * P].bitcast(FP8X4),
                            lhsT_scale=scales[:, c0 + g * P:c0 + (g + 1) * P],
                            rhs=w_words[:, g * COLS:(g + 1) * COLS].bitcast(FP8X4),
                            rhs_scale=w_scales[:, g * COLS:(g + 1) * COLS],
                            start=(g == 0),
                            stop=(g == 1),
                        )
                n = n0 + j0
                s, g0, t_count = group_of[n]
                if n == g0:
                    out_sb[s] = opool.tile([P, E * t_count * R], F32, name="out%d" % s, tag="out%d" % s)
                ov = out_sb[s][:].rearrange("p (e t r) -> p e t r", e=E, r=R)
                dst = ov[:, :, n - g0:n - g0 + pair, :]
                src = acc[:, 0:pair * COLS].rearrange("p (t e r) -> p e t r", t=pair, r=R)
                if i == last and j0 == 0:
                    nc.vector.tensor_copy(out=dst, in_=src)
                else:
                    nc.scalar.copy(out=dst, in_=src)
                if n + pair == g0 + t_count:
                    for e in range(E):
                        nc.sync.dma_start(
                            out=of[e][g0 * P:(g0 + t_count) * P, :].rearrange("(p t) r -> p t r", t=t_count),
                            in_=ov[:, e, :, :],
                        )

        w_raw = const.tile([P, 2 * D], BF16, name="w_raw")
        nc.sync.dma_start(
            out=w_raw[:].rearrange("p (h k) -> p h k", h=2),
            in_=wf.rearrange("(h p) k -> p h k", p=P),
        )
        load_chunks()

        ident = const.tile([P, P], F32, name="ident")
        make_identity(nc, ident[:])

        def prepare_weights():
            w_raw_words = w_raw[:].bitcast(F32)
            wg = w_grouped[:].bitcast(F32).rearrange("p (g c u) -> p g c u", g=2, u=2)
            nc.scalar.copy(out=wg[:, :, 0:P, :], in_=transpose_tile(w_raw_words, 0, 1))
            nc.vector.tensor_copy(out=wg[:, :, P:2 * P, :], in_=transpose_tile(w_raw_words, WORDS, 1))

        def quantise_weights():
            nc.vector.quantize_mx(out=w_words[:].bitcast(FP8X4), scales=w_scales[:], in_=w_grouped[:])

        w_grouped = const.tile([P, 2 * COLS * 4], BF16, name="w_grouped", align_bytes=64)
        w_words = const.tile([P, 2 * COLS], U32, name="w_words", align_bytes=64)
        w_scales = const.tile([P, 2 * COLS], U8, name="w_scales", align_bytes=64)
        prepare_weights()
        quantise_weights()
        sort_unit(0)
        multiplied = 0
        for i in range(last + 2):
            if i < last:
                sort_unit(i + 1)
            if i >= 1:
                quantise_unit(i - 1)
            if i <= last:
                transpose_unit(i)
            behind = 2 if i < last else 1
            while multiplied <= i - behind:
                multiply_unit(multiplied)
                multiplied += 1
